import numpy as np
import ml_dtypes


def mxq(x, axis, fmt="e4m3"):
    dtype, down = {"e4m3": (ml_dtypes.float8_e4m3fn, 7), "e5m2": (ml_dtypes.float8_e5m2, 14)}[fmt]
    v = np.moveaxis(np.asarray(x, np.float32).astype(ml_dtypes.bfloat16).astype(np.float64), axis, -1)
    blocks = v.reshape(v.shape[:-1] + (-1, 32))
    amax = np.abs(blocks).max(-1, keepdims=True)
    byte = np.maximum(np.where(amax > 0, np.frexp(amax)[1] - 1 + 127, 0) - down, 1)
    scale = np.exp2(byte - 127.0)
    codes = (blocks / scale).astype(np.float32).astype(dtype).astype(np.float64)
    return np.moveaxis((codes * scale).reshape(v.shape), -1, axis)


WIDE = False


def mx_kscale(k):
    if not WIDE:
        return np.ones(k)
    levels = np.array([10, -10, 5, -5, 0])
    if k % 512:
        return np.exp2(np.random.permutation(np.resize(levels, k // 32))).repeat(32)
    a = np.empty((k // 512, 16))
    for p in range(k // 512):
        a[p, :8] = np.random.permutation(np.resize(levels, 8))
        for g in range(8):
            far = levels[np.abs(levels - a[p, g]) >= 10]
            a[p, g + 8] = far[np.random.randint(len(far))]
    return np.exp2(a.ravel()).repeat(32)


BF16 = ml_dtypes.bfloat16


def bf(x):
    return np.asarray(x, np.float32).astype(BF16)


def f64(x):
    return np.asarray(x).astype(np.float64)


B, C, P, NH, NW = 4, 8, 8, 32, 32
D = C * P * P
QK_SCALE = 1.0


def rel_bias(p):
    i = np.arange(p, dtype=np.float64)
    down = np.exp(-i / (p / 2))[:, None] * np.ones((1, p))
    right = down.T
    br = np.exp(-(i[:, None] + i[None, :]) / (p / 2))
    return np.stack([
        np.rot90(br, 2), np.flip(down, 0), np.rot90(br, 1),
        np.flip(right, 1), np.ones((p, p)), right,
        np.rot90(br, 3), down, br,
    ], axis=0)


def setup_inputs():
    s = mx_kscale(D)
    sx = np.tile(s.reshape(C, P, P), (1, NH, NW))
    return {"x": bf(np.random.standard_normal((B, C, NH * P, NW * P)) * sx),
            "W_qkv": bf(np.random.standard_normal((3 * D, D)) / np.sqrt(D) / s),
            "b_qkv": bf(np.random.standard_normal(3 * D) * 0.5)}


def reference(x, W_qkv, b_qkv):
    p, c = P, C
    b, _, h, w = x.shape
    nh, nw = h // p, w // p
    feat = f64(x).reshape(b, c, nh, p, nw, p).transpose(0, 2, 4, 1, 3, 5).reshape(b, nh, nw, c * p * p)
    y = mxq(feat, 3, "e4m3") @ mxq(f64(W_qkv), 1, "e4m3").T
    qkv = np.pad(y, ((0, 0), (1, 1), (1, 1), (0, 0))) + f64(b_qkv)
    qkv = qkv.reshape(b, nh + 2, nw + 2, 3, c, p, p)
    core_q = qkv[:, 1:nh + 1, 1:nw + 1, 0] * QK_SCALE
    k = np.stack([qkv[:, di:di + nh, dj:dj + nw, 1] for di in range(3) for dj in range(3)], axis=3)
    v = np.stack([qkv[:, di:di + nh, dj:dj + nw, 2] for di in range(3) for dj in range(3)], axis=3)
    bias = rel_bias(p)
    attn = core_q[:, :, :, None] * k * bias[:, None]
    out = np.sum(attn * v, axis=3)
    return out.transpose(0, 3, 1, 4, 2, 5).reshape(b, c, nh * p, nw * p)

@@ -1,0 +1,382 @@
+from contextlib import ExitStack
+
+import concourse.mybir as mybir
+from concourse.masks import make_identity
+
+F32 = mybir.dt.float32
+BF16 = mybir.dt.bfloat16
+U32 = mybir.dt.uint32
+U8 = mybir.dt.uint8
+FP8X4 = mybir.dt.float8_e4m3fn_x4
+ADD = mybir.AluOpType.add
+MULT = mybir.AluOpType.mult
+IDENTITY = mybir.ActivationFunctionType.Identity
+EXP = mybir.ActivationFunctionType.Exp
+COPY = mybir.ActivationFunctionType.Copy
+
+FLOPS = 2 * 4096 * 512 * 1536
+
+P = 128
+NB = 4
+NJ = 32
+NG = 8
+NF = 4
+ROW = 132
+LAST_STORES = {3: 0, 5: 16, 6: 24, 7: 28}
+
+
+def tile_attentionconv_t_kernel(tc, x, W_qkv, b_qkv, out):
+    nc = tc.nc
+    with ExitStack() as ctx:
+        keep = ctx.enter_context(tc.tile_pool(name="keep", bufs=1))
+        work = ctx.enter_context(tc.tile_pool(name="work", bufs=2))
+        psum = ctx.enter_context(tc.psum_pool(name="psum", bufs=2))
+        ctx.enter_context(tc.manual_schedule())
+
+        ident = keep.tile([P, P], F32, name="ident")
+        make_identity(nc, ident[:])
+        zero = keep.tile([P, ROW], F32, name="zero")
+        nc.vector.memset(zero[:], 0.0)
+        zs = keep.tile([P, P], F32, name="zs")
+        zr = keep.tile([P, P], F32, name="zr")
+        for t in range(8):
+            nc.vector.memset(zs[:].rearrange("p (a s) -> p a s", s=8)[:, :, t : t + 1], float(-t))
+            nc.gpsimd.memset(zr[:].rearrange("p (c r s) -> p c r s", c=2, r=8)[:, :, t : t + 1, :], float(-t))
+        bz = keep.tile([P, P], BF16, name="bz")
+        nc.vector.memset(bz[:], 0.0)
+        nc.sync.dma_start(out=bz[0:12, :], in_=b_qkv.rearrange("(s p) -> s p", p=P))
+
+        w_sb = keep.tile([P, 12 * 512], BF16, name="w_sb")
+        w_view = W_qkv.rearrange("(t f p) e -> f p t e", t=3, f=NF, p=P)
+
+        def load_w(fb):
+            nc.sync.dma_start(
+                out=w_sb[:, fb * 1536 : (fb + 1) * 1536].rearrange("p (t e) -> p t e", t=3), in_=w_view[fb]
+            )
+
+        load_w(0)
+        xs = work.tile([P, 16384], BF16, name="xs", tag="big", bufs=2)
+        for cp in range(4):
+            for b in range(NB):
+                nc.sync.dma_start(
+                    out=xs[b:P:4, cp * 4096 : (cp + 1) * 4096].rearrange("p (c f) -> p c f", c=2),
+                    in_=x[b, 2 * cp : 2 * cp + 2].rearrange("c (i r) w -> i c (r w)", r=8),
+                )
+        for fb in range(1, NF):
+            load_w(fb)
+
+        bzf = keep.tile([P, P], F32, name="bzf")
+        nc.vector.tensor_copy(out=bzf[:], in_=bz[:])
+        cps = psum.tile([P, 512], F32, name="cps", tag="tp", bufs=2)
+        nc.tensor.transpose(cps[:, 0:P], zs[:], ident[:])
+        nc.tensor.transpose(cps[:, P : 2 * P], zr[:], ident[:])
+        bps = psum.tile([P, 512], F32, name="bps", tag="tp", bufs=2)
+        nc.tensor.transpose(bps[:, 0:P], bzf[:], ident[:])
+        consts = keep.tile([P, 12], F32, name="consts")
+        nc.vector.tensor_copy(out=consts[:, 0:12], in_=bps[:, 0:12])
+        expo = keep.tile([P, 4], F32, name="expo")
+        nc.vector.tensor_copy(
+            out=expo[:, 0:2].unsqueeze(2), in_=cps[:, 0 : 2 * P].rearrange("p (w c) -> p w c", c=P)[:, :, 0:1]
+        )
+        nc.vector.tensor_scalar(
+            out=expo[:, 2:4], in0=expo[:, 0:2], scalar1=-1.0, scalar2=-7.0, op0=MULT, op1=ADD
+        )
+        wts = keep.tile([P, 4], F32, name="wts")
+        nc.scalar.activation(out=wts[:], in_=expo[:], func=EXP, scale=0.25)
+        a2s = wts[:, 0:1]
+        a2r = wts[:, 1:2]
+        a0s = wts[:, 2:3]
+        a0r = wts[:, 3:4]
+        cc = keep.tile([P, 8], F32, name="cc")
+        wsum = keep.tile([P, 1], F32, name="wsum")
+        nc.vector.tensor_tensor(out=cc[:, 0:4], in0=consts[:, 4:8], in1=consts[:, 8:12], op=MULT)
+        nc.vector.tensor_tensor(out=wsum[:], in0=a0s, in1=a2s, op=ADD)
+        nc.vector.tensor_scalar_add(out=wsum[:], in0=wsum[:], scalar1=1.0)
+        nc.vector.tensor_scalar_mul(out=cc[:, 4:8], in0=cc[:, 0:4], scalar1=wsum[:])
+
+        wc = keep.tile([P, 12 * P], U32, name="wc", align_bytes=64)
+        wsc = keep.tile([P, 12 * P], U8, name="wsc", align_bytes=64)
+        w_words = w_sb[:].bitcast(F32)
+
+        gw_of = {}
+
+        def w_transpose(fb, eng_copy):
+            gw = work.tile([P, 1536], BF16, name="gw", tag="gw", bufs=2, align_bytes=64)
+            gw_of[fb] = gw
+            gww = gw[:].bitcast(F32).rearrange("p (t o u) -> p t o u", t=3, o=P, u=2)
+            for t0, nt in ((0, 2), (2, 1)):
+                tp = psum.tile([P, 512], F32, name="tpw", tag="tp", bufs=2)
+                for t in range(nt):
+                    for u in range(2):
+                        c0 = (3 * fb + t0 + t) * 256
+                        nc.tensor.transpose(
+                            tp[:, (2 * t + u) * P : (2 * t + u + 1) * P], w_words[:, c0 + u : c0 + 256 : 2], ident[:]
+                        )
+                eng_copy(
+                    out=gww[:, t0 : t0 + nt],
+                    in_=tp[:, 0 : nt * 256].rearrange("p (t u o) -> p t o u", t=nt, u=2),
+                )
+
+        def w_quantise(fb):
+            gw = gw_of[fb]
+            for t in range(3):
+                s = (3 * fb + t) * P
+                nc.vector.quantize_mx(
+                    out=wc[:, s : s + P].bitcast(FP8X4),
+                    scales=wsc[:, s : s + P],
+                    in_=gw[:, t * 512 : (t + 1) * 512],
+                )
+
+        w_transpose(0, nc.vector.tensor_copy)
+        w_quantise(0)
+
+        xg = work.tile([P, 8192], F32, name="xg", tag="big", bufs=2)
+        xs_words = xs[:].bitcast(F32).rearrange("p (q j w u) -> p q j w u", q=64, j=NJ, w=2, u=2)
+        xg_view = xg[:].rearrange("p (j u q w) -> p j u q w", j=NJ, u=2, q=64, w=2)
+        for cp in range(4):
+            for jq in range(4):
+                eng_copy = nc.vector.tensor_copy if jq % 2 == 0 else nc.scalar.copy
+                eng_copy(
+                    out=xg_view[:, 8 * jq : 8 * jq + 8, :, 16 * cp : 16 * cp + 16, :],
+                    in_=xs_words[:, 16 * cp : 16 * cp + 16, 8 * jq : 8 * jq + 8].rearrange("p q j w u -> p j u q w"),
+                )
+        xc = keep.tile([P, 4096], U32, name="xc", align_bytes=64)
+        xsc = keep.tile([P, 4096], U8, name="xsc", align_bytes=64)
+
+        gx_of = {}
+        tpx_of = {}
+
+        def x_transpose(g):
+            for h in range(2):
+                tp = psum.tile([P, 512], F32, name="tpx", tag="tp", bufs=2)
+                tpx_of[(g, h)] = tp
+                for jj in range(2):
+                    for u in range(2):
+                        c0 = (4 * g + 2 * h + jj) * 256 + u * P
+                        nc.tensor.transpose(
+                            tp[:, (2 * jj + u) * P : (2 * jj + u + 1) * P], xg[:, c0 : c0 + P], ident[:]
+                        )
+
+        def x_copy(g):
+            gx = work.tile([P, 2048], BF16, name="gx", tag="gx", bufs=3, align_bytes=64)
+            gx_of[g] = gx
+            gxw = gx[:].bitcast(F32).rearrange("p (h jj c u) -> p h jj c u", h=2, jj=2, c=P, u=2)
+            for h in range(2):
+                nc.scalar.copy(
+                    out=gxw[:, h], in_=tpx_of[(g, h)][:].rearrange("p (jj u c) -> p jj c u", jj=2, u=2)
+                )
+
+        def x_quantise(g):
+            nc.vector.quantize_mx(
+                out=xc[:, 512 * g : 512 * g + 512].bitcast(FP8X4),
+                scales=xsc[:, 512 * g : 512 * g + 512],
+                in_=gx_of[g][:],
+            )
+
+        def project(dst, slot, g):
+            nc.tensor.matmul_mx(
+                out=dst,
+                lhsT=wc[:, slot * P : (slot + 1) * P].bitcast(FP8X4),
+                lhsT_scale=wsc[:, slot * P : (slot + 1) * P],
+                rhs=xc[:, 512 * g : 512 * g + 512].bitcast(FP8X4),
+                rhs_scale=xsc[:, 512 * g : 512 * g + 512],
+                start=True,
+                stop=True,
+            )
+
+        kv_of = {}
+        hj_of = {}
+        os_of = {}
+
+        def begin_block(fb):
+            kv = work.tile([P, 34 * P], F32, name="kv", tag="kv", bufs=2)
+            hj = work.tile([P, 33 * ROW], F32, name="hj", tag="hj", bufs=2)
+            ost = work.tile([P, 4096], F32, name="ost", tag="big", bufs=2)
+            kv_of[fb] = kv
+            hj_of[fb] = hj
+            os_of[fb] = ost
+            for s in (0, 33):
+                nc.scalar.activation(
+                    out=kv[:, s * P : (s + 1) * P], in_=zero[:, 0:P], func=IDENTITY, bias=cc[:, fb : fb + 1], scale=1.0
+                )
+            nc.scalar.activation(
+                out=hj[:].rearrange("p (j c) -> p j c", c=ROW)[:, :, 0:4],
+                in_=zero[:].rearrange("p (j c) -> p j c", c=4),
+                func=IDENTITY,
+                bias=cc[:, 4 + fb : 5 + fb],
+                scale=1.0,
+            )
+
+        units = [(fb, g) for fb in range(NF) for g in range(NG)]
+        n_units = len(units)
+        tiles = {}
+
+        def hwin(u, off):
+            fb, g = units[u]
+            return hj_of[fb][:, off : off + NJ * ROW].rearrange("p (j c) -> p j c", c=ROW)[:, 4 * g : 4 * g + 4, 0:P]
+
+        def kwin(u, s):
+            fb, g = units[u]
+            return kv_of[fb][:, (4 * g + s) * P : (4 * g + s + 4) * P].rearrange("p (j c) -> p j c", c=P)
+
+        def pe_project(u):
+            fb, g = units[u]
+            vps = psum.tile([P, 512], F32, name="vps", tag="vps", bufs=1)
+            kps = psum.tile([P, 512], F32, name="kps", tag="kps", bufs=1)
+            qps = psum.tile([P, 512], F32, name="qps", tag="qps", bufs=1)
+            tiles[("v", u)] = vps
+            tiles[("k", u)] = kps
+            tiles[("q", u)] = qps
+            project(vps[:], 3 * fb + 2, g)
+            project(kps[:], 3 * fb + 1, g)
+            project(qps[:], 3 * fb, g)
+
+        def act_v_q(u):
+            fb, g = units[u]
+            vt = work.tile([P, 512], F32, name="vt", tag="vt", bufs=2)
+            qs = work.tile([P, 512], F32, name="qs", tag="qs", bufs=2)
+            tiles[("vt", u)] = vt
+            tiles[("qs", u)] = qs
+            nc.scalar.activation(
+                out=vt[:], in_=tiles[("v", u)][:], func=IDENTITY, bias=consts[:, 8 + fb : 9 + fb], scale=1.0
+            )
+            nc.scalar.activation(
+                out=qs[:], in_=tiles[("q", u)][:], func=IDENTITY, bias=consts[:, fb : fb + 1], scale=1.0
+            )
+
+        def dve_kv(u):
+            fb, g = units[u]
+            nc.vector.scalar_tensor_tensor(
+                out=kv_of[fb][:, (1 + 4 * g) * P : (5 + 4 * g) * P],
+                in0=tiles[("k", u)][:],
+                scalar=consts[:, 4 + fb : 5 + fb],
+                in1=tiles[("vt", u)][:],
+                op0=ADD,
+                op1=MULT,
+            )
+
+        def pe_q_transpose(u):
+            qtp = psum.tile([P, 512], F32, name="qtp", tag="qtp", bufs=1)
+            tiles[("qtp", u)] = qtp
+            qs = tiles[("qs", u)]
+            for jj in range(4):
+                nc.tensor.transpose(qtp[:, jj * P : (jj + 1) * P], qs[:, jj * P : (jj + 1) * P], ident[:])
+
+        def act_q_copy(u):
+            qts = work.tile([P, 512], F32, name="qts", tag="qts", bufs=6)
+            tiles[("qts", u)] = qts
+            nc.scalar.copy(
+                out=qts[:].rearrange("p (q jj s) -> p q jj s", q=16, jj=4, s=8),
+                in_=tiles[("qtp", u)][:].rearrange("p (jj q s) -> p q jj s", jj=4, q=16, s=8),
+            )
+
+        def dve_columns(u):
+            nc.vector.scalar_tensor_tensor(
+                out=hwin(u, 4), in0=kwin(u, 0), scalar=a0s, in1=kwin(u, 1), op0=MULT, op1=ADD
+            )
+            nc.vector.scalar_tensor_tensor(
+                out=hwin(u, 4), in0=kwin(u, 2), scalar=a2s, in1=hwin(u, 4), op0=MULT, op1=ADD
+            )
+
+        def act_scale_up(u):
+            t0 = work.tile([P, 512], F32, name="t0", tag="t0", bufs=3)
+            tiles[("t0", u)] = t0
+            nc.scalar.activation(out=t0[:].rearrange("p (j c) -> p j c", c=P), in_=hwin(u, 0), func=COPY, scale=a0r)
+
+        def dve_scale_down(u):
+            t2 = work.tile([P, 512], F32, name="t2", tag="t2", bufs=3)
+            tiles[("t2", u)] = t2
+            nc.vector.tensor_scalar_mul(out=t2[:].rearrange("p (j c) -> p j c", c=P), in0=hwin(u, 8), scalar1=a2r)
+
+        def pe_rows(u):
+            fb, g = units[u]
+            stp = psum.tile([P, 512], F32, name="stp", tag="stp", bufs=2)
+            tiles[("stp", u)] = stp
+            t0 = tiles[("t0", u)]
+            t2 = tiles[("t2", u)]
+            for jj in range(4):
+                dst = stp[:, jj * P : (jj + 1) * P]
+                c0 = (4 * g + jj) * ROW + 4
+                nc.tensor.matmul(
+                    out=dst, lhsT=hj_of[fb][:, c0 : c0 + P], rhs=ident[:], is_transpose=True, start=True, stop=False
+                )
+                nc.tensor.matmul(
+                    out=dst, lhsT=t0[:, jj * P : (jj + 1) * P], rhs=ident[:], is_transpose=True, start=False, stop=False
+                )
+                nc.tensor.matmul(
+                    out=dst, lhsT=t2[:, jj * P : (jj + 1) * P], rhs=ident[:], is_transpose=True, start=False, stop=True
+                )
+
+        def store(fb, ja, jb):
+            if ja == 0 and jb == NJ:
+                for b in range(NB):
+                    nc.sync.dma_start(
+                        out=out[b, 2 * fb : 2 * fb + 2].rearrange("c (i r) w -> i c (r w)", r=8),
+                        in_=os_of[fb][b:P:4, :].rearrange("p (c f) -> p c f", c=2),
+                    )
+            else:
+                for b in range(NB):
+                    for c in range(2):
+                        nc.sync.dma_start(
+                            out=out[b, 2 * fb + c].rearrange("(i r) w -> i r w", r=8)[:, :, 8 * ja : 8 * jb],
+                            in_=os_of[fb][b:P:4, c * 2048 : (c + 1) * 2048].rearrange("p (r w) -> p r w", r=8)[
+                                :, :, 8 * ja : 8 * jb
+                            ],
+                        )
+
+        def dve_final(u):
+            fb, g = units[u]
+            j0 = 4 * g
+            nc.vector.tensor_tensor(
+                out=os_of[fb][:].rearrange("p (q j s) -> p q j s", q=16, j=NJ, s=8)[:, :, j0 : j0 + 4, :],
+                in0=tiles[("stp", u)][:].rearrange("p (jj q s) -> p q jj s", jj=4, q=16, s=8),
+                in1=tiles[("qts", u)][:].rearrange("p (q jj s) -> p q jj s", q=16, jj=4, s=8),
+                op=MULT,
+            )
+            if fb < NF - 1:
+                if g == NG - 1:
+                    store(fb, 0, NJ)
+            elif g in LAST_STORES:
+                store(fb, LAST_STORES[g], j0 + 4)
+
+        def live(u):
+            return 0 <= u < n_units
+
+        for g in range(3):
+            x_transpose(g)
+            x_copy(g)
+            if g >= 1:
+                x_quantise(g - 1)
+        for s in range(-1, n_units + 3):
+            if live(s - 1):
+                dve_scale_down(s - 1)
+            if live(s + 1):
+                if units[s + 1][1] == 0:
+                    begin_block(units[s + 1][0])
+                pe_project(s + 1)
+            if live(s - 3):
+                dve_final(s - 3)
+            if live(s + 1):
+                act_v_q(s + 1)
+            if live(s - 2):
+                pe_rows(s - 2)
+            if live(s + 1):
+                dve_kv(s + 1)
+            if live(s - 1):
+                act_scale_up(s - 1)
+            if live(s + 1):
+                pe_q_transpose(s + 1)
+            if 0 <= s + 3 < NG and s + 3 >= 3:
+                x_transpose(s + 3)
+            if live(s):
+                dve_columns(s)
+            if 0 <= s + 2 < NG and s + 2 >= 2:
+                x_quantise(s + 2)
+            if live(s) and units[s][1] == 5 and units[s][0] + 1 < NF:
+                w_quantise(units[s][0] + 1)
+            if live(s + 1):
+                act_q_copy(s + 1)
+            if 0 <= s + 3 < NG and s + 3 >= 3:
+                x_copy(s + 3)
+            if live(s) and units[s][1] == 3 and units[s][0] + 1 < NF:
+                w_transpose(units[s][0] + 1, nc.scalar.copy)

@@ -222,19 +222,19 @@ def tile_attentionconv_t_kernel(tc, x, W_qkv, b_qkv, out):
         def pe_project(u):
             fb, g = units[u]
             vps = psum.tile([P, 512], F32, name="vps", tag="vps", bufs=1)
-            kps = psum.tile([P, 512], F32, name="kps", tag="kps", bufs=1)
+            kps = psum.tile([P, 512], F32, name="kps", tag="kps", bufs=2)
             qps = psum.tile([P, 512], F32, name="qps", tag="qps", bufs=1)
             tiles[("v", u)] = vps
             tiles[("k", u)] = kps
             tiles[("q", u)] = qps
             project(vps[:], 3 * fb + 2, g)
-            project(kps[:], 3 * fb + 1, g)
             project(qps[:], 3 * fb, g)
+            project(kps[:], 3 * fb + 1, g)
 
         def act_v_q(u):
             fb, g = units[u]
-            vt = work.tile([P, 512], F32, name="vt", tag="vt", bufs=2)
-            qs = work.tile([P, 512], F32, name="qs", tag="qs", bufs=2)
+            vt = work.tile([P, 512], F32, name="vt", tag="vt", bufs=3)
+            qs = work.tile([P, 512], F32, name="qs", tag="qs", bufs=3)
             tiles[("vt", u)] = vt
             tiles[("qs", u)] = qs
             nc.scalar.activation(
@@ -256,7 +256,7 @@ def tile_attentionconv_t_kernel(tc, x, W_qkv, b_qkv, out):
             )
 
         def pe_q_transpose(u):
-            qtp = psum.tile([P, 512], F32, name="qtp", tag="qtp", bufs=1)
+            qtp = psum.tile([P, 512], F32, name="qtp", tag="tp", bufs=2)
             tiles[("qtp", u)] = qtp
             qs = tiles[("qs", u)]
             for jj in range(4):
@@ -270,10 +270,12 @@ def tile_attentionconv_t_kernel(tc, x, W_qkv, b_qkv, out):
                 in_=tiles[("qtp", u)][:].rearrange("p (jj q s) -> p q jj s", jj=4, q=16, s=8),
             )
 
-        def dve_columns(u):
+        def dve_columns_left(u):
             nc.vector.scalar_tensor_tensor(
                 out=hwin(u, 4), in0=kwin(u, 0), scalar=a0s, in1=kwin(u, 1), op0=MULT, op1=ADD
             )
+
+        def dve_columns_right(u):
             nc.vector.scalar_tensor_tensor(
                 out=hwin(u, 4), in0=kwin(u, 2), scalar=a2s, in1=hwin(u, 4), op0=MULT, op1=ADD
             )
@@ -348,34 +350,34 @@ def tile_attentionconv_t_kernel(tc, x, W_qkv, b_qkv, out):
             if g >= 1:
                 x_quantise(g - 1)
         for s in range(-1, n_units + 3):
-            if live(s - 1):
-                dve_scale_down(s - 1)
             if live(s + 1):
                 if units[s + 1][1] == 0:
                     begin_block(units[s + 1][0])
                 pe_project(s + 1)
+            if live(s - 1):
+                dve_columns_right(s - 1)
+            if live(s):
+                dve_columns_left(s)
             if live(s - 3):
                 dve_final(s - 3)
             if live(s + 1):
                 act_v_q(s + 1)
-            if live(s - 2):
-                pe_rows(s - 2)
-            if live(s + 1):
                 dve_kv(s + 1)
+            if live(s):
+                pe_q_transpose(s)
             if live(s - 1):
                 act_scale_up(s - 1)
-            if live(s + 1):
-                pe_q_transpose(s + 1)
+                dve_scale_down(s - 1)
+            if live(s - 2):
+                pe_rows(s - 2)
             if 0 <= s + 3 < NG and s + 3 >= 3:
                 x_transpose(s + 3)
-            if live(s):
-                dve_columns(s)
             if 0 <= s + 2 < NG and s + 2 >= 2:
                 x_quantise(s + 2)
             if live(s) and units[s][1] == 5 and units[s][0] + 1 < NF:
                 w_quantise(units[s][0] + 1)
-            if live(s + 1):
-                act_q_copy(s + 1)
+            if live(s):
+                act_q_copy(s)
             if 0 <= s + 3 < NG and s + 3 >= 3:
                 x_copy(s + 3)
             if live(s) and units[s][1] == 3 and units[s][0] + 1 < NF:

@@ -285,10 +285,12 @@ def tile_attentionconv_t_kernel(tc, x, W_qkv, b_qkv, out):
             tiles[("t0", u)] = t0
             nc.scalar.activation(out=t0[:].rearrange("p (j c) -> p j c", c=P), in_=hwin(u, 0), func=COPY, scale=a0r)
 
-        def dve_scale_down(u):
+        def gps_scale_down(u):
             t2 = work.tile([P, 512], F32, name="t2", tag="t2", bufs=3)
             tiles[("t2", u)] = t2
-            nc.vector.tensor_scalar_mul(out=t2[:].rearrange("p (j c) -> p j c", c=P), in0=hwin(u, 8), scalar1=a2r)
+            nc.gpsimd.tensor_scalar(
+                out=t2[:].rearrange("p (j c) -> p j c", c=P), in0=hwin(u, 8), scalar1=a2r, scalar2=0.0, op0=MULT, op1=ADD
+            )
 
         def pe_rows(u):
             fb, g = units[u]
@@ -367,7 +369,7 @@ def tile_attentionconv_t_kernel(tc, x, W_qkv, b_qkv, out):
                 pe_q_transpose(s)
             if live(s - 1):
                 act_scale_up(s - 1)
-                dve_scale_down(s - 1)
+                gps_scale_down(s - 1)
             if live(s - 2):
                 pe_rows(s - 2)
             if 0 <= s + 3 < NG and s + 3 >= 3:

@@ -19,10 +19,15 @@ FLOPS = 2 * 4096 * 512 * 1536
 P = 128
 NB = 4
 NJ = 32
-NG = 8
 NF = 4
-ROW = 132
-LAST_STORES = {3: 0, 5: 16, 6: 24, 7: 28}
+PAD = 8
+ROW = PAD + P
+X_CHUNKS = ((0, 2), (2, 2), (4, 2), (6, 1), (7, 1))
+HEAD_WIDTHS = (2, 2, 4, 4, 4, 4, 4, 4, 4)
+BODY_WIDTHS = (4, 4, 4, 4, 4, 4, 4, 4)
+TAIL_WIDTHS = (4, 4, 4, 4, 4, 4, 4, 2, 2)
+STORES = {16: 0, 32: 16}
+LAST_STORES = {16: 0, 24: 16, 28: 24, 32: 28}
 
 
 def tile_attentionconv_t_kernel(tc, x, W_qkv, b_qkv, out):
@@ -33,19 +38,9 @@ def tile_attentionconv_t_kernel(tc, x, W_qkv, b_qkv, out):
         psum = ctx.enter_context(tc.psum_pool(name="psum", bufs=2))
         ctx.enter_context(tc.manual_schedule())
 
-        ident = keep.tile([P, P], F32, name="ident")
-        make_identity(nc, ident[:])
-        zero = keep.tile([P, ROW], F32, name="zero")
-        nc.vector.memset(zero[:], 0.0)
-        zs = keep.tile([P, P], F32, name="zs")
-        zr = keep.tile([P, P], F32, name="zr")
-        for t in range(8):
-            nc.vector.memset(zs[:].rearrange("p (a s) -> p a s", s=8)[:, :, t : t + 1], float(-t))
-            nc.gpsimd.memset(zr[:].rearrange("p (c r s) -> p c r s", c=2, r=8)[:, :, t : t + 1, :], float(-t))
         bz = keep.tile([P, P], BF16, name="bz")
         nc.vector.memset(bz[:], 0.0)
-        nc.sync.dma_start(out=bz[0:12, :], in_=b_qkv.rearrange("(s p) -> s p", p=P))
-
+        nc.scalar.dma_start(out=bz[0:12, :], in_=b_qkv.rearrange("(s p) -> s p", p=P))
         w_sb = keep.tile([P, 12 * 512], BF16, name="w_sb")
         w_view = W_qkv.rearrange("(t f p) e -> f p t e", t=3, f=NF, p=P)
 
@@ -55,16 +50,27 @@ def tile_attentionconv_t_kernel(tc, x, W_qkv, b_qkv, out):
             )
 
         load_w(0)
-        xs = work.tile([P, 16384], BF16, name="xs", tag="big", bufs=2)
-        for cp in range(4):
+        xs_of = []
+        for c0, nch in X_CHUNKS:
+            xs = keep.tile([P, nch * 2048], BF16, name=f"xs{c0}")
+            xs_of.append(xs)
             for b in range(NB):
                 nc.sync.dma_start(
-                    out=xs[b:P:4, cp * 4096 : (cp + 1) * 4096].rearrange("p (c f) -> p c f", c=2),
-                    in_=x[b, 2 * cp : 2 * cp + 2].rearrange("c (i r) w -> i c (r w)", r=8),
+                    out=xs[b:P:4, :].rearrange("p (c f) -> p c f", c=nch),
+                    in_=x[b, c0 : c0 + nch].rearrange("c (i r) w -> i c (r w)", r=8),
                 )
         for fb in range(1, NF):
             load_w(fb)
 
+        ident = keep.tile([P, P], F32, name="ident")
+        make_identity(nc, ident[:])
+        zero = keep.tile([P, 33 * PAD], F32, name="zero")
+        nc.vector.memset(zero[:], 0.0)
+        zs = keep.tile([P, P], F32, name="zs")
+        zr = keep.tile([P, P], F32, name="zr")
+        for t in range(8):
+            nc.vector.memset(zs[:].rearrange("p (a s) -> p a s", s=8)[:, :, t : t + 1], float(-t))
+            nc.gpsimd.memset(zr[:].rearrange("p (c r s) -> p c r s", c=2, r=8)[:, :, t : t + 1, :], float(-t))
         bzf = keep.tile([P, P], F32, name="bzf")
         nc.vector.tensor_copy(out=bzf[:], in_=bz[:])
         cps = psum.tile([P, 512], F32, name="cps", tag="tp", bufs=2)
@@ -72,21 +78,19 @@ def tile_attentionconv_t_kernel(tc, x, W_qkv, b_qkv, out):
         nc.tensor.transpose(cps[:, P : 2 * P], zr[:], ident[:])
         bps = psum.tile([P, 512], F32, name="bps", tag="tp", bufs=2)
         nc.tensor.transpose(bps[:, 0:P], bzf[:], ident[:])
-        consts = keep.tile([P, 12], F32, name="consts")
-        nc.vector.tensor_copy(out=consts[:, 0:12], in_=bps[:, 0:12])
         expo = keep.tile([P, 4], F32, name="expo")
         nc.vector.tensor_copy(
             out=expo[:, 0:2].unsqueeze(2), in_=cps[:, 0 : 2 * P].rearrange("p (w c) -> p w c", c=P)[:, :, 0:1]
         )
-        nc.vector.tensor_scalar(
-            out=expo[:, 2:4], in0=expo[:, 0:2], scalar1=-1.0, scalar2=-7.0, op0=MULT, op1=ADD
-        )
+        nc.vector.tensor_scalar(out=expo[:, 2:4], in0=expo[:, 0:2], scalar1=-1.0, scalar2=-7.0, op0=MULT, op1=ADD)
         wts = keep.tile([P, 4], F32, name="wts")
         nc.scalar.activation(out=wts[:], in_=expo[:], func=EXP, scale=0.25)
         a2s = wts[:, 0:1]
         a2r = wts[:, 1:2]
         a0s = wts[:, 2:3]
         a0r = wts[:, 3:4]
+        consts = keep.tile([P, 12], F32, name="consts")
+        nc.vector.tensor_copy(out=consts[:, 0:12], in_=bps[:, 0:12])
         cc = keep.tile([P, 8], F32, name="cc")
         wsum = keep.tile([P, 1], F32, name="wsum")
         nc.vector.tensor_tensor(out=cc[:, 0:4], in0=consts[:, 4:8], in1=consts[:, 8:12], op=MULT)
@@ -100,7 +104,7 @@ def tile_attentionconv_t_kernel(tc, x, W_qkv, b_qkv, out):
 
         gw_of = {}
 
-        def w_transpose(fb, eng_copy):
+        def w_transpose(fb):
             gw = work.tile([P, 1536], BF16, name="gw", tag="gw", bufs=2, align_bytes=64)
             gw_of[fb] = gw
             gww = gw[:].bitcast(F32).rearrange("p (t o u) -> p t o u", t=3, o=P, u=2)
@@ -112,7 +116,7 @@ def tile_attentionconv_t_kernel(tc, x, W_qkv, b_qkv, out):
                         nc.tensor.transpose(
                             tp[:, (2 * t + u) * P : (2 * t + u + 1) * P], w_words[:, c0 + u : c0 + 256 : 2], ident[:]
                         )
-                eng_copy(
+                nc.scalar.copy(
                     out=gww[:, t0 : t0 + nt],
                     in_=tp[:, 0 : nt * 256].rearrange("p (t u o) -> p t o u", t=nt, u=2),
                 )
@@ -127,61 +131,65 @@ def tile_attentionconv_t_kernel(tc, x, W_qkv, b_qkv, out):
                     in_=gw[:, t * 512 : (t + 1) * 512],
                 )
 
-        w_transpose(0, nc.vector.tensor_copy)
+        w_transpose(0)
         w_quantise(0)
 
-        xg = work.tile([P, 8192], F32, name="xg", tag="big", bufs=2)
-        xs_words = xs[:].bitcast(F32).rearrange("p (q j w u) -> p q j w u", q=64, j=NJ, w=2, u=2)
+        units = []
+        for fb in range(NF):
+            ja = 0
+            for nj in HEAD_WIDTHS if fb == 0 else TAIL_WIDTHS if fb == NF - 1 else BODY_WIDTHS:
+                units.append((fb, ja, ja + nj))
+                ja += nj
+        n_units = len(units)
+        n_x = len(HEAD_WIDTHS)
+        tiles = {}
+
+        def live(u):
+            return 0 <= u < n_units
+
+        xg = keep.tile([P, 8192], F32, name="xg")
         xg_view = xg[:].rearrange("p (j u q w) -> p j u q w", j=NJ, u=2, q=64, w=2)
-        for cp in range(4):
-            for jq in range(4):
-                eng_copy = nc.vector.tensor_copy if jq % 2 == 0 else nc.scalar.copy
-                eng_copy(
-                    out=xg_view[:, 8 * jq : 8 * jq + 8, :, 16 * cp : 16 * cp + 16, :],
-                    in_=xs_words[:, 16 * cp : 16 * cp + 16, 8 * jq : 8 * jq + 8].rearrange("p q j w u -> p j u q w"),
-                )
+
+        def regroup(chunk, ja, jb):
+            c0, nch = X_CHUNKS[chunk]
+            xs_words = xs_of[chunk][:].bitcast(F32).rearrange("p (q j w u) -> p q j w u", q=8 * nch, j=NJ, w=2, u=2)
+            nc.vector.tensor_copy(
+                out=xg_view[:, ja:jb, :, 8 * c0 : 8 * (c0 + nch), :],
+                in_=xs_words[:, :, ja:jb].rearrange("p q j w u -> p j u q w"),
+            )
+
         xc = keep.tile([P, 4096], U32, name="xc", align_bytes=64)
         xsc = keep.tile([P, 4096], U8, name="xsc", align_bytes=64)
 
-        gx_of = {}
-        tpx_of = {}
-
-        def x_transpose(g):
-            for h in range(2):
+        def x_transpose(u):
+            ja, jb = units[u][1:]
+            for j0 in range(ja, jb, 2):
                 tp = psum.tile([P, 512], F32, name="tpx", tag="tp", bufs=2)
-                tpx_of[(g, h)] = tp
+                tiles[("tpx", u, j0)] = tp
                 for jj in range(2):
-                    for u in range(2):
-                        c0 = (4 * g + 2 * h + jj) * 256 + u * P
+                    for h in range(2):
+                        c0 = (j0 + jj) * 256 + h * P
                         nc.tensor.transpose(
-                            tp[:, (2 * jj + u) * P : (2 * jj + u + 1) * P], xg[:, c0 : c0 + P], ident[:]
+                            tp[:, (2 * jj + h) * P : (2 * jj + h + 1) * P], xg[:, c0 : c0 + P], ident[:]
                         )
 
-        def x_copy(g):
-            gx = work.tile([P, 2048], BF16, name="gx", tag="gx", bufs=3, align_bytes=64)
-            gx_of[g] = gx
+        def x_copy(u, *engines):
+            ja, jb = units[u][1:]
+            gx = work.tile([P, 2048], BF16, name="gx", tag="gx", bufs=2, align_bytes=64)
+            tiles[("gx", u)] = gx
             gxw = gx[:].bitcast(F32).rearrange("p (h jj c u) -> p h jj c u", h=2, jj=2, c=P, u=2)
-            for h in range(2):
-                nc.scalar.copy(
-                    out=gxw[:, h], in_=tpx_of[(g, h)][:].rearrange("p (jj u c) -> p jj c u", jj=2, u=2)
+            for h in range((jb - ja) // 2):
+                engines[h](
+                    out=gxw[:, h],
+                    in_=tiles[("tpx", u, ja + 2 * h)][:].rearrange("p (jj u c) -> p jj c u", jj=2, u=2),
                 )
 
-        def x_quantise(g):
+        def x_quantise(u):
+            ja, jb = units[u][1:]
             nc.vector.quantize_mx(
-                out=xc[:, 512 * g : 512 * g + 512].bitcast(FP8X4),
-                scales=xsc[:, 512 * g : 512 * g + 512],
-                in_=gx_of[g][:],
-            )
-
-        def project(dst, slot, g):
-            nc.tensor.matmul_mx(
-                out=dst,
-                lhsT=wc[:, slot * P : (slot + 1) * P].bitcast(FP8X4),
-                lhsT_scale=wsc[:, slot * P : (slot + 1) * P],
-                rhs=xc[:, 512 * g : 512 * g + 512].bitcast(FP8X4),
-                rhs_scale=xsc[:, 512 * g : 512 * g + 512],
-                start=True,
-                stop=True,
+                out=xc[:, P * ja : P * jb].bitcast(FP8X4),
+                scales=xsc[:, P * ja : P * jb],
+                in_=tiles[("gx", u)][:, 0 : 512 * (jb - ja)],
             )
 
         kv_of = {}
@@ -191,66 +199,71 @@ def tile_attentionconv_t_kernel(tc, x, W_qkv, b_qkv, out):
         def begin_block(fb):
             kv = work.tile([P, 34 * P], F32, name="kv", tag="kv", bufs=2)
             hj = work.tile([P, 33 * ROW], F32, name="hj", tag="hj", bufs=2)
-            ost = work.tile([P, 4096], F32, name="ost", tag="big", bufs=2)
             kv_of[fb] = kv
             hj_of[fb] = hj
-            os_of[fb] = ost
             for s in (0, 33):
-                nc.scalar.activation(
-                    out=kv[:, s * P : (s + 1) * P], in_=zero[:, 0:P], func=IDENTITY, bias=cc[:, fb : fb + 1], scale=1.0
+                nc.gpsimd.tensor_scalar(
+                    out=kv[:, s * P : (s + 1) * P],
+                    in0=zero[:, 0:P],
+                    scalar1=cc[:, fb : fb + 1],
+                    scalar2=0.0,
+                    op0=ADD,
+                    op1=ADD,
                 )
-            nc.scalar.activation(
-                out=hj[:].rearrange("p (j c) -> p j c", c=ROW)[:, :, 0:4],
-                in_=zero[:].rearrange("p (j c) -> p j c", c=4),
-                func=IDENTITY,
-                bias=cc[:, 4 + fb : 5 + fb],
-                scale=1.0,
+            nc.gpsimd.tensor_scalar(
+                out=hj[:].rearrange("p (j c) -> p j c", c=ROW)[:, :, 0:PAD],
+                in0=zero[:].rearrange("p (j c) -> p j c", c=PAD),
+                scalar1=cc[:, 4 + fb : 5 + fb],
+                scalar2=0.0,
+                op0=ADD,
+                op1=ADD,
             )
-
-        units = [(fb, g) for fb in range(NF) for g in range(NG)]
-        n_units = len(units)
-        tiles = {}
 
         def hwin(u, off):
-            fb, g = units[u]
-            return hj_of[fb][:, off : off + NJ * ROW].rearrange("p (j c) -> p j c", c=ROW)[:, 4 * g : 4 * g + 4, 0:P]
+            fb, ja, jb = units[u]
+            return hj_of[fb][:, off : off + NJ * ROW].rearrange("p (j c) -> p j c", c=ROW)[:, ja:jb, 0:P]
 
         def kwin(u, s):
-            fb, g = units[u]
-            return kv_of[fb][:, (4 * g + s) * P : (4 * g + s + 4) * P].rearrange("p (j c) -> p j c", c=P)
+            fb, ja, jb = units[u]
+            return kv_of[fb][:, (ja + s) * P : (jb + s) * P].rearrange("p (j c) -> p j c", c=P)
+
+        def width(u):
+            return P * (units[u][2] - units[u][1])
 
         def pe_project(u):
-            fb, g = units[u]
-            vps = psum.tile([P, 512], F32, name="vps", tag="vps", bufs=1)
-            kps = psum.tile([P, 512], F32, name="kps", tag="kps", bufs=2)
-            qps = psum.tile([P, 512], F32, name="qps", tag="qps", bufs=1)
-            tiles[("v", u)] = vps
-            tiles[("k", u)] = kps
-            tiles[("q", u)] = qps
-            project(vps[:], 3 * fb + 2, g)
-            project(qps[:], 3 * fb, g)
-            project(kps[:], 3 * fb + 1, g)
+            fb, ja, jb = units[u]
+            for what, third, bufs in (("v", 2, 1), ("q", 0, 1), ("k", 1, 2)):
+                ps = psum.tile([P, 512], F32, name=what + "ps", tag=what + "ps", bufs=bufs)
+                tiles[(what, u)] = ps
+                w0 = (3 * fb + third) * P
+                nc.tensor.matmul_mx(
+                    out=ps[:, 0 : width(u)],
+                    lhsT=wc[:, w0 : w0 + P].bitcast(FP8X4),
+                    lhsT_scale=wsc[:, w0 : w0 + P],
+                    rhs=xc[:, P * ja : P * jb].bitcast(FP8X4),
+                    rhs_scale=xsc[:, P * ja : P * jb],
+                    start=True,
+                    stop=True,
+                )
 
         def act_v_q(u):
-            fb, g = units[u]
-            vt = work.tile([P, 512], F32, name="vt", tag="vt", bufs=3)
-            qs = work.tile([P, 512], F32, name="qs", tag="qs", bufs=3)
-            tiles[("vt", u)] = vt
-            tiles[("qs", u)] = qs
-            nc.scalar.activation(
-                out=vt[:], in_=tiles[("v", u)][:], func=IDENTITY, bias=consts[:, 8 + fb : 9 + fb], scale=1.0
-            )
-            nc.scalar.activation(
-                out=qs[:], in_=tiles[("q", u)][:], func=IDENTITY, bias=consts[:, fb : fb + 1], scale=1.0
-            )
+            fb = units[u][0]
+            n = width(u)
+            for what, c in (("v", 8 + fb), ("q", fb)):
+                t = work.tile([P, 512], F32, name=what + "t", tag=what + "t", bufs=3)
+                tiles[(what + "t", u)] = t
+                nc.scalar.activation(
+                    out=t[:, 0:n], in_=tiles[(what, u)][:, 0:n], func=IDENTITY, bias=consts[:, c : c + 1], scale=1.0
+                )
 
         def dve_kv(u):
-            fb, g = units[u]
+            fb, ja, jb = units[u]
+            n = width(u)
             nc.vector.scalar_tensor_tensor(
-                out=kv_of[fb][:, (1 + 4 * g) * P : (5 + 4 * g) * P],
-                in0=tiles[("k", u)][:],
+                out=kv_of[fb][:, (1 + ja) * P : (1 + jb) * P],
+                in0=tiles[("k", u)][:, 0:n],
                 scalar=consts[:, 4 + fb : 5 + fb],
-                in1=tiles[("vt", u)][:],
+                in1=tiles[("vt", u)][:, 0:n],
                 op0=ADD,
                 op1=MULT,
             )
@@ -258,99 +271,105 @@ def tile_attentionconv_t_kernel(tc, x, W_qkv, b_qkv, out):
         def pe_q_transpose(u):
             qtp = psum.tile([P, 512], F32, name="qtp", tag="tp", bufs=2)
             tiles[("qtp", u)] = qtp
-            qs = tiles[("qs", u)]
-            for jj in range(4):
-                nc.tensor.transpose(qtp[:, jj * P : (jj + 1) * P], qs[:, jj * P : (jj + 1) * P], ident[:])
+            for c0 in range(0, width(u), P):
+                nc.tensor.transpose(qtp[:, c0 : c0 + P], tiles[("qt", u)][:, c0 : c0 + P], ident[:])
 
         def act_q_copy(u):
-            qts = work.tile([P, 512], F32, name="qts", tag="qts", bufs=6)
+            qts = work.tile([P, 512], F32, name="qts", tag="qts", bufs=5)
             tiles[("qts", u)] = qts
+            n = width(u)
             nc.scalar.copy(
-                out=qts[:].rearrange("p (q jj s) -> p q jj s", q=16, jj=4, s=8),
-                in_=tiles[("qtp", u)][:].rearrange("p (jj q s) -> p q jj s", jj=4, q=16, s=8),
+                out=qts[:, 0:n].rearrange("p (q jj s) -> p q jj s", q=16, s=8),
+                in_=tiles[("qtp", u)][:, 0:n].rearrange("p (jj q s) -> p q jj s", q=16, s=8),
             )
 
         def dve_columns_left(u):
             nc.vector.scalar_tensor_tensor(
-                out=hwin(u, 4), in0=kwin(u, 0), scalar=a0s, in1=kwin(u, 1), op0=MULT, op1=ADD
+                out=hwin(u, PAD), in0=kwin(u, 0), scalar=a0s, in1=kwin(u, 1), op0=MULT, op1=ADD
             )
 
         def dve_columns_right(u):
             nc.vector.scalar_tensor_tensor(
-                out=hwin(u, 4), in0=kwin(u, 2), scalar=a2s, in1=hwin(u, 4), op0=MULT, op1=ADD
+                out=hwin(u, PAD), in0=kwin(u, 2), scalar=a2s, in1=hwin(u, PAD), op0=MULT, op1=ADD
             )
 
         def act_scale_up(u):
-            t0 = work.tile([P, 512], F32, name="t0", tag="t0", bufs=3)
+            t0 = work.tile([P, 512], F32, name="t0", tag="t0", bufs=2)
             tiles[("t0", u)] = t0
-            nc.scalar.activation(out=t0[:].rearrange("p (j c) -> p j c", c=P), in_=hwin(u, 0), func=COPY, scale=a0r)
+            nc.scalar.activation(
+                out=t0[:, 0 : width(u)].rearrange("p (j c) -> p j c", c=P), in_=hwin(u, PAD - 4), func=COPY, scale=a0r
+            )
 
         def gps_scale_down(u):
-            t2 = work.tile([P, 512], F32, name="t2", tag="t2", bufs=3)
+            t2 = work.tile([P, 512], F32, name="t2", tag="t2", bufs=2)
             tiles[("t2", u)] = t2
             nc.gpsimd.tensor_scalar(
-                out=t2[:].rearrange("p (j c) -> p j c", c=P), in0=hwin(u, 8), scalar1=a2r, scalar2=0.0, op0=MULT, op1=ADD
+                out=t2[:, 0 : width(u)].rearrange("p (j c) -> p j c", c=P),
+                in0=hwin(u, PAD + 4),
+                scalar1=a2r,
+                scalar2=0.0,
+                op0=MULT,
+                op1=ADD,
             )
 
         def pe_rows(u):
-            fb, g = units[u]
+            fb, ja, jb = units[u]
             stp = psum.tile([P, 512], F32, name="stp", tag="stp", bufs=2)
             tiles[("stp", u)] = stp
             t0 = tiles[("t0", u)]
             t2 = tiles[("t2", u)]
-            for jj in range(4):
-                dst = stp[:, jj * P : (jj + 1) * P]
-                c0 = (4 * g + jj) * ROW + 4
-                nc.tensor.matmul(
-                    out=dst, lhsT=hj_of[fb][:, c0 : c0 + P], rhs=ident[:], is_transpose=True, start=True, stop=False
-                )
-                nc.tensor.matmul(
-                    out=dst, lhsT=t0[:, jj * P : (jj + 1) * P], rhs=ident[:], is_transpose=True, start=False, stop=False
-                )
-                nc.tensor.matmul(
-                    out=dst, lhsT=t2[:, jj * P : (jj + 1) * P], rhs=ident[:], is_transpose=True, start=False, stop=True
-                )
+            for jj in range(jb - ja):
+                cols = slice(jj * P, (jj + 1) * P)
+                c0 = (ja + jj) * ROW + PAD
+                for n, src in enumerate((hj_of[fb][:, c0 : c0 + P], t0[:, cols], t2[:, cols])):
+                    nc.tensor.matmul(
+                        out=stp[:, cols], lhsT=src, rhs=ident[:], is_transpose=True, start=n == 0, stop=n == 2
+                    )
 
         def store(fb, ja, jb):
-            if ja == 0 and jb == NJ:
-                for b in range(NB):
+            ost = os_of[(fb, ja // 16)]
+            for b in range(NB):
+                for c in range(2):
                     nc.sync.dma_start(
-                        out=out[b, 2 * fb : 2 * fb + 2].rearrange("c (i r) w -> i c (r w)", r=8),
-                        in_=os_of[fb][b:P:4, :].rearrange("p (c f) -> p c f", c=2),
+                        out=out[b, 2 * fb + c].rearrange("(i r) w -> i r w", r=8)[:, :, 8 * ja : 8 * jb],
+                        in_=ost[b:P:4, c * 1024 : (c + 1) * 1024].rearrange("p (r w) -> p r w", r=8)[
+                            :, :, 8 * (ja % 16) : 8 * (ja % 16 + jb - ja)
+                        ],
                     )
-            else:
-                for b in range(NB):
-                    for c in range(2):
-                        nc.sync.dma_start(
-                            out=out[b, 2 * fb + c].rearrange("(i r) w -> i r w", r=8)[:, :, 8 * ja : 8 * jb],
-                            in_=os_of[fb][b:P:4, c * 2048 : (c + 1) * 2048].rearrange("p (r w) -> p r w", r=8)[
-                                :, :, 8 * ja : 8 * jb
-                            ],
-                        )
 
         def dve_final(u):
-            fb, g = units[u]
-            j0 = 4 * g
+            fb, ja, jb = units[u]
+            n = width(u)
+            if ja % 16 == 0:
+                ost = work.tile([P, 2048], F32, name="ost", tag="ost", bufs=2)
+                os_of[(fb, ja // 16)] = ost
             nc.vector.tensor_tensor(
-                out=os_of[fb][:].rearrange("p (q j s) -> p q j s", q=16, j=NJ, s=8)[:, :, j0 : j0 + 4, :],
-                in0=tiles[("stp", u)][:].rearrange("p (jj q s) -> p q jj s", jj=4, q=16, s=8),
-                in1=tiles[("qts", u)][:].rearrange("p (q jj s) -> p q jj s", q=16, jj=4, s=8),
+                out=os_of[(fb, ja // 16)][:].rearrange("p (q j s) -> p q j s", q=16, s=8)[
+                    :, :, ja % 16 : ja % 16 + jb - ja, :
+                ],
+                in0=tiles[("stp", u)][:, 0:n].rearrange("p (jj q s) -> p q jj s", q=16, s=8),
+                in1=tiles[("qts", u)][:, 0:n].rearrange("p (q jj s) -> p q jj s", q=16, s=8),
                 op=MULT,
             )
-            if fb < NF - 1:
-                if g == NG - 1:
-                    store(fb, 0, NJ)
-            elif g in LAST_STORES:
-                store(fb, LAST_STORES[g], j0 + 4)
+            stores = LAST_STORES if fb == NF - 1 else STORES
+            if jb in stores:
+                store(fb, stores[jb], jb)
 
-        def live(u):
-            return 0 <= u < n_units
+        last = len(X_CHUNKS) - 1
+        for chunk in range(last):
+            regroup(chunk, 0, NJ)
+        regroup(last, 0, 2)
+        x_transpose(0)
+        x_copy(0, nc.scalar.copy)
+        regroup(last, 2, 8)
+        x_transpose(1)
+        x_copy(1, nc.scalar.copy)
+        x_quantise(0)
+        regroup(last, 8, NJ)
+        x_transpose(2)
+        x_copy(2, nc.scalar.copy, nc.vector.tensor_copy)
+        x_quantise(1)
 
-        for g in range(3):
-            x_transpose(g)
-            x_copy(g)
-            if g >= 1:
-                x_quantise(g - 1)
         for s in range(-1, n_units + 3):
             if live(s + 1):
                 if units[s + 1][1] == 0:
@@ -372,15 +391,15 @@ def tile_attentionconv_t_kernel(tc, x, W_qkv, b_qkv, out):
                 gps_scale_down(s - 1)
             if live(s - 2):
                 pe_rows(s - 2)
-            if 0 <= s + 3 < NG and s + 3 >= 3:
+            if 3 <= s + 3 < n_x:
                 x_transpose(s + 3)
-            if 0 <= s + 2 < NG and s + 2 >= 2:
+            if 2 <= s + 2 < n_x:
                 x_quantise(s + 2)
-            if live(s) and units[s][1] == 5 and units[s][0] + 1 < NF:
+            if live(s) and units[s][0] + 1 < NF and units[s][2] == 28:
                 w_quantise(units[s][0] + 1)
             if live(s):
                 act_q_copy(s)
-            if 0 <= s + 3 < NG and s + 3 >= 3:
-                x_copy(s + 3)
-            if live(s) and units[s][1] == 3 and units[s][0] + 1 < NF:
-                w_transpose(units[s][0] + 1, nc.scalar.copy)
+            if 3 <= s + 3 < n_x:
+                x_copy(s + 3, nc.scalar.copy, nc.vector.tensor_copy if s < 2 else nc.scalar.copy)
+            if live(s) and units[s][0] + 1 < NF and units[s][2] == 24:
+                w_transpose(units[s][0] + 1)

@@ -71,13 +71,9 @@ def tile_attentionconv_t_kernel(tc, x, W_qkv, b_qkv, out):
         for t in range(8):
             nc.vector.memset(zs[:].rearrange("p (a s) -> p a s", s=8)[:, :, t : t + 1], float(-t))
             nc.gpsimd.memset(zr[:].rearrange("p (c r s) -> p c r s", c=2, r=8)[:, :, t : t + 1, :], float(-t))
-        bzf = keep.tile([P, P], F32, name="bzf")
-        nc.vector.tensor_copy(out=bzf[:], in_=bz[:])
         cps = psum.tile([P, 512], F32, name="cps", tag="tp", bufs=2)
         nc.tensor.transpose(cps[:, 0:P], zs[:], ident[:])
         nc.tensor.transpose(cps[:, P : 2 * P], zr[:], ident[:])
-        bps = psum.tile([P, 512], F32, name="bps", tag="tp", bufs=2)
-        nc.tensor.transpose(bps[:, 0:P], bzf[:], ident[:])
         expo = keep.tile([P, 4], F32, name="expo")
         nc.vector.tensor_copy(
             out=expo[:, 0:2].unsqueeze(2), in_=cps[:, 0 : 2 * P].rearrange("p (w c) -> p w c", c=P)[:, :, 0:1]
@@ -89,14 +85,6 @@ def tile_attentionconv_t_kernel(tc, x, W_qkv, b_qkv, out):
         a2r = wts[:, 1:2]
         a0s = wts[:, 2:3]
         a0r = wts[:, 3:4]
-        consts = keep.tile([P, 12], F32, name="consts")
-        nc.vector.tensor_copy(out=consts[:, 0:12], in_=bps[:, 0:12])
-        cc = keep.tile([P, 8], F32, name="cc")
-        wsum = keep.tile([P, 1], F32, name="wsum")
-        nc.vector.tensor_tensor(out=cc[:, 0:4], in0=consts[:, 4:8], in1=consts[:, 8:12], op=MULT)
-        nc.vector.tensor_tensor(out=wsum[:], in0=a0s, in1=a2s, op=ADD)
-        nc.vector.tensor_scalar_add(out=wsum[:], in0=wsum[:], scalar1=1.0)
-        nc.vector.tensor_scalar_mul(out=cc[:, 4:8], in0=cc[:, 0:4], scalar1=wsum[:])
 
         wc = keep.tile([P, 12 * P], U32, name="wc", align_bytes=64)
         wsc = keep.tile([P, 12 * P], U8, name="wsc", align_bytes=64)
@@ -192,6 +180,23 @@ def tile_attentionconv_t_kernel(tc, x, W_qkv, b_qkv, out):
                 in_=tiles[("gx", u)][:, 0 : 512 * (jb - ja)],
             )
 
+        last = len(X_CHUNKS) - 1
+        regroup(0, 0, NJ)
+        bzf = keep.tile([P, P], F32, name="bzf")
+        nc.vector.tensor_copy(out=bzf[:], in_=bz[:])
+        bps = psum.tile([P, 512], F32, name="bps", tag="tp", bufs=2)
+        nc.tensor.transpose(bps[:, 0:P], bzf[:], ident[:])
+        consts = keep.tile([P, 12], F32, name="consts")
+        nc.vector.tensor_copy(out=consts[:, 0:12], in_=bps[:, 0:12])
+        cc = keep.tile([P, 8], F32, name="cc")
+        wsum = keep.tile([P, 1], F32, name="wsum")
+        nc.vector.tensor_tensor(out=cc[:, 0:4], in0=consts[:, 4:8], in1=consts[:, 8:12], op=MULT)
+        nc.vector.tensor_tensor(out=wsum[:], in0=a0s, in1=a2s, op=ADD)
+        nc.vector.tensor_scalar_add(out=wsum[:], in0=wsum[:], scalar1=1.0)
+        nc.vector.tensor_scalar_mul(out=cc[:, 4:8], in0=cc[:, 0:4], scalar1=wsum[:])
+        for chunk in range(1, last):
+            regroup(chunk, 0, NJ)
+
         kv_of = {}
         hj_of = {}
         os_of = {}
@@ -205,17 +210,17 @@ def tile_attentionconv_t_kernel(tc, x, W_qkv, b_qkv, out):
                 nc.gpsimd.tensor_scalar(
                     out=kv[:, s * P : (s + 1) * P],
                     in0=zero[:, 0:P],
-                    scalar1=cc[:, fb : fb + 1],
-                    scalar2=0.0,
-                    op0=ADD,
+                    scalar1=a2r,
+                    scalar2=cc[:, fb : fb + 1],
+                    op0=MULT,
                     op1=ADD,
                 )
             nc.gpsimd.tensor_scalar(
                 out=hj[:].rearrange("p (j c) -> p j c", c=ROW)[:, :, 0:PAD],
                 in0=zero[:].rearrange("p (j c) -> p j c", c=PAD),
-                scalar1=cc[:, 4 + fb : 5 + fb],
-                scalar2=0.0,
-                op0=ADD,
+                scalar1=a2r,
+                scalar2=cc[:, 4 + fb : 5 + fb],
+                op0=MULT,
                 op1=ADD,
             )
 
@@ -355,9 +360,6 @@ def tile_attentionconv_t_kernel(tc, x, W_qkv, b_qkv, out):
             if jb in stores:
                 store(fb, stores[jb], jb)
 
-        last = len(X_CHUNKS) - 1
-        for chunk in range(last):
-            regroup(chunk, 0, NJ)
         regroup(last, 0, 2)
         x_transpose(0)
         x_copy(0, nc.scalar.copy)

@@ -196,6 +196,10 @@ def tile_attentionconv_t_kernel(tc, x, W_qkv, b_qkv, out):
         nc.vector.tensor_scalar_mul(out=cc[:, 4:8], in0=cc[:, 0:4], scalar1=wsum[:])
         for chunk in range(1, last):
             regroup(chunk, 0, NJ)
+        bqp = psum.tile([P, 512], F32, name="bqp", tag="tp", bufs=2)
+        nc.tensor.transpose(bqp[:, 0:P], consts[:, 0:1].to_broadcast([P, P]), ident[:])
+        bq = keep.tile([P, P], F32, name="bq")
+        nc.scalar.copy(out=bq[:], in_=bqp[:, 0:P])
 
         kv_of = {}
         hj_of = {}
@@ -207,21 +211,15 @@ def tile_attentionconv_t_kernel(tc, x, W_qkv, b_qkv, out):
             kv_of[fb] = kv
             hj_of[fb] = hj
             for s in (0, 33):
-                nc.gpsimd.tensor_scalar(
-                    out=kv[:, s * P : (s + 1) * P],
-                    in0=zero[:, 0:P],
-                    scalar1=a2r,
-                    scalar2=cc[:, fb : fb + 1],
-                    op0=MULT,
-                    op1=ADD,
+                nc.scalar.activation(
+                    out=kv[:, s * P : (s + 1) * P], in_=zero[:, 0:P], func=IDENTITY, bias=cc[:, fb : fb + 1], scale=1.0
                 )
-            nc.gpsimd.tensor_scalar(
+            nc.scalar.activation(
                 out=hj[:].rearrange("p (j c) -> p j c", c=ROW)[:, :, 0:PAD],
-                in0=zero[:].rearrange("p (j c) -> p j c", c=PAD),
-                scalar1=a2r,
-                scalar2=cc[:, 4 + fb : 5 + fb],
-                op0=MULT,
-                op1=ADD,
+                in_=zero[:].rearrange("p (j c) -> p j c", c=PAD),
+                func=IDENTITY,
+                bias=cc[:, 4 + fb : 5 + fb],
+                scale=1.0,
             )
 
         def hwin(u, off):
@@ -235,26 +233,38 @@ def tile_attentionconv_t_kernel(tc, x, W_qkv, b_qkv, out):
         def width(u):
             return P * (units[u][2] - units[u][1])
 
+        def mx(dst, lhsT, lhsT_scale, rhs, rhs_scale):
+            nc.tensor.matmul_mx(
+                out=dst,
+                lhsT=lhsT.bitcast(FP8X4),
+                lhsT_scale=lhsT_scale,
+                rhs=rhs.bitcast(FP8X4),
+                rhs_scale=rhs_scale,
+                start=True,
+                stop=True,
+            )
+
+        def direct(u):
+            return units[u][0] == 0 and u % 2 == 1
+
         def pe_project(u):
             fb, ja, jb = units[u]
             for what, third, bufs in (("v", 2, 1), ("q", 0, 1), ("k", 1, 2)):
                 ps = psum.tile([P, 512], F32, name=what + "ps", tag=what + "ps", bufs=bufs)
                 tiles[(what, u)] = ps
-                w0 = (3 * fb + third) * P
-                nc.tensor.matmul_mx(
-                    out=ps[:, 0 : width(u)],
-                    lhsT=wc[:, w0 : w0 + P].bitcast(FP8X4),
-                    lhsT_scale=wsc[:, w0 : w0 + P],
-                    rhs=xc[:, P * ja : P * jb].bitcast(FP8X4),
-                    rhs_scale=xsc[:, P * ja : P * jb],
-                    start=True,
-                    stop=True,
-                )
+                w = slice((3 * fb + third) * P, (3 * fb + third + 1) * P)
+                if what == "q" and direct(u):
+                    for j in range(ja, jb):
+                        c = slice(P * j, P * (j + 1))
+                        mx(ps[:, P * (j - ja) : P * (j - ja + 1)], xc[:, c], xsc[:, c], wc[:, w], wsc[:, w])
+                else:
+                    c = slice(P * ja, P * jb)
+                    mx(ps[:, 0 : width(u)], wc[:, w], wsc[:, w], xc[:, c], xsc[:, c])
 
         def act_v_q(u):
             fb = units[u][0]
             n = width(u)
-            for what, c in (("v", 8 + fb), ("q", fb)):
+            for what, c in (("v", 8 + fb), ("q", fb))[: 1 if direct(u) else 2]:
                 t = work.tile([P, 512], F32, name=what + "t", tag=what + "t", bufs=3)
                 tiles[(what + "t", u)] = t
                 nc.scalar.activation(
@@ -278,6 +288,21 @@ def tile_attentionconv_t_kernel(tc, x, W_qkv, b_qkv, out):
             tiles[("qtp", u)] = qtp
             for c0 in range(0, width(u), P):
                 nc.tensor.transpose(qtp[:, c0 : c0 + P], tiles[("qt", u)][:, c0 : c0 + P], ident[:])
+
+        def dve_q_bias(u):
+            fb = units[u][0]
+            qts = work.tile([P, 512], F32, name="qts", tag="qts", bufs=5)
+            tiles[("qts", u)] = qts
+            n = width(u)
+            nc.vector.tensor_tensor(
+                out=qts[:, 0:n].rearrange("p (q jj s) -> p q jj s", q=16, s=8),
+                in0=tiles[("q", u)][:, 0:n].rearrange("p (jj q s) -> p q jj s", q=16, s=8),
+                in1=bq[:, fb * P : (fb + 1) * P]
+                .rearrange("p (q s) -> p q s", s=8)
+                .unsqueeze(2)
+                .to_broadcast([P, 16, n // P, 8]),
+                op=ADD,
+            )
 
         def act_q_copy(u):
             qts = work.tile([P, 512], F32, name="qts", tag="qts", bufs=5)
@@ -386,7 +411,9 @@ def tile_attentionconv_t_kernel(tc, x, W_qkv, b_qkv, out):
             if live(s + 1):
                 act_v_q(s + 1)
                 dve_kv(s + 1)
-            if live(s):
+                if direct(s + 1):
+                    dve_q_bias(s + 1)
+            if live(s) and not direct(s):
                 pe_q_transpose(s)
             if live(s - 1):
                 act_scale_up(s - 1)
@@ -399,7 +426,7 @@ def tile_attentionconv_t_kernel(tc, x, W_qkv, b_qkv, out):
                 x_quantise(s + 2)
             if live(s) and units[s][0] + 1 < NF and units[s][2] == 28:
                 w_quantise(units[s][0] + 1)
-            if live(s):
+            if live(s) and not direct(s):
                 act_q_copy(s)
             if 3 <= s + 3 < n_x:
                 x_copy(s + 3, nc.scalar.copy, nc.vector.tensor_copy if s < 2 else nc.scalar.copy)

from contextlib import ExitStack

import concourse.mybir as mybir
from concourse.masks import make_identity

F32 = mybir.dt.float32
BF16 = mybir.dt.bfloat16
U32 = mybir.dt.uint32
U8 = mybir.dt.uint8
FP8X4 = mybir.dt.float8_e4m3fn_x4
ADD = mybir.AluOpType.add
MULT = mybir.AluOpType.mult
IDENTITY = mybir.ActivationFunctionType.Identity
EXP = mybir.ActivationFunctionType.Exp
COPY = mybir.ActivationFunctionType.Copy

FLOPS = 2 * 4096 * 512 * 1536

P = 128
NB = 4
NJ = 32
NF = 4
PAD = 8
ROW = PAD + P
X_CHUNKS = ((0, 2), (2, 2), (4, 2), (6, 1), (7, 1))
HEAD_WIDTHS = (2, 2, 4, 4, 4, 4, 4, 4, 4)
BODY_WIDTHS = (4, 4, 4, 4, 4, 4, 4, 4)
TAIL_WIDTHS = (4, 4, 4, 4, 4, 4, 4, 2, 2)
STORES = {16: 0, 32: 16}
LAST_STORES = {16: 0, 24: 16, 28: 24, 32: 28}


def tile_attentionconv_t_kernel(tc, x, W_qkv, b_qkv, out):
    nc = tc.nc
    with ExitStack() as ctx:
        keep = ctx.enter_context(tc.tile_pool(name="keep", bufs=1))
        work = ctx.enter_context(tc.tile_pool(name="work", bufs=2))
        psum = ctx.enter_context(tc.psum_pool(name="psum", bufs=2))
        ctx.enter_context(tc.manual_schedule())

        bz = keep.tile([P, P], BF16, name="bz")
        nc.vector.memset(bz[:], 0.0)
        nc.scalar.dma_start(out=bz[0:12, :], in_=b_qkv.rearrange("(s p) -> s p", p=P))
        w_sb = keep.tile([P, 12 * 512], BF16, name="w_sb")
        w_view = W_qkv.rearrange("(t f p) e -> f p t e", t=3, f=NF, p=P)

        def load_w(fb):
            nc.sync.dma_start(
                out=w_sb[:, fb * 1536 : (fb + 1) * 1536].rearrange("p (t e) -> p t e", t=3), in_=w_view[fb]
            )

        load_w(0)
        xs_of = []
        for c0, nch in X_CHUNKS:
            xs = keep.tile([P, nch * 2048], BF16, name=f"xs{c0}")
            xs_of.append(xs)
            for b in range(NB):
                nc.sync.dma_start(
                    out=xs[b:P:4, :].rearrange("p (c f) -> p c f", c=nch),
                    in_=x[b, c0 : c0 + nch].rearrange("c (i r) w -> i c (r w)", r=8),
                )
        for fb in range(1, NF):
            load_w(fb)

        ident = keep.tile([P, P], F32, name="ident")
        make_identity(nc, ident[:])
        zero = keep.tile([P, 33 * PAD], F32, name="zero")
        nc.vector.memset(zero[:], 0.0)
        zs = keep.tile([P, P], F32, name="zs")
        zr = keep.tile([P, P], F32, name="zr")
        for t in range(8):
            nc.vector.memset(zs[:].rearrange("p (a s) -> p a s", s=8)[:, :, t : t + 1], float(-t))
            nc.gpsimd.memset(zr[:].rearrange("p (c r s) -> p c r s", c=2, r=8)[:, :, t : t + 1, :], float(-t))
        cps = psum.tile([P, 512], F32, name="cps", tag="tp", bufs=2)
        nc.tensor.transpose(cps[:, 0:P], zs[:], ident[:])
        nc.tensor.transpose(cps[:, P : 2 * P], zr[:], ident[:])
        expo = keep.tile([P, 4], F32, name="expo")
        nc.vector.tensor_copy(
            out=expo[:, 0:2].unsqueeze(2), in_=cps[:, 0 : 2 * P].rearrange("p (w c) -> p w c", c=P)[:, :, 0:1]
        )
        nc.vector.tensor_scalar(out=expo[:, 2:4], in0=expo[:, 0:2], scalar1=-1.0, scalar2=-7.0, op0=MULT, op1=ADD)
        wts = keep.tile([P, 4], F32, name="wts")
        nc.scalar.activation(out=wts[:], in_=expo[:], func=EXP, scale=0.25)
        a2s = wts[:, 0:1]
        a2r = wts[:, 1:2]
        a0s = wts[:, 2:3]
        a0r = wts[:, 3:4]

        wc = keep.tile([P, 12 * P], U32, name="wc", align_bytes=64)
        wsc = keep.tile([P, 12 * P], U8, name="wsc", align_bytes=64)
        w_words = w_sb[:].bitcast(F32)

        gw_of = {}

        def w_transpose(fb):
            gw = work.tile([P, 1536], BF16, name="gw", tag="gw", bufs=2, align_bytes=64)
            gw_of[fb] = gw
            gww = gw[:].bitcast(F32).rearrange("p (t o u) -> p t o u", t=3, o=P, u=2)
            for t0, nt in ((0, 2), (2, 1)):
                tp = psum.tile([P, 512], F32, name="tpw", tag="tp", bufs=2)
                for t in range(nt):
                    for u in range(2):
                        c0 = (3 * fb + t0 + t) * 256
                        nc.tensor.transpose(
                            tp[:, (2 * t + u) * P : (2 * t + u + 1) * P], w_words[:, c0 + u : c0 + 256 : 2], ident[:]
                        )
                nc.scalar.copy(
                    out=gww[:, t0 : t0 + nt],
                    in_=tp[:, 0 : nt * 256].rearrange("p (t u o) -> p t o u", t=nt, u=2),
                )

        def w_quantise(fb):
            gw = gw_of[fb]
            for t in range(3):
                s = (3 * fb + t) * P
                nc.vector.quantize_mx(
                    out=wc[:, s : s + P].bitcast(FP8X4),
                    scales=wsc[:, s : s + P],
                    in_=gw[:, t * 512 : (t + 1) * 512],
                )

        w_transpose(0)
        w_quantise(0)

        units = []
        for fb in range(NF):
            ja = 0
            for nj in HEAD_WIDTHS if fb == 0 else TAIL_WIDTHS if fb == NF - 1 else BODY_WIDTHS:
                units.append((fb, ja, ja + nj))
                ja += nj
        n_units = len(units)
        n_x = len(HEAD_WIDTHS)
        tiles = {}

        def live(u):
            return 0 <= u < n_units

        xg = keep.tile([P, 8192], F32, name="xg")
        xg_view = xg[:].rearrange("p (j u q w) -> p j u q w", j=NJ, u=2, q=64, w=2)

        def regroup(chunk, ja, jb):
            c0, nch = X_CHUNKS[chunk]
            xs_words = xs_of[chunk][:].bitcast(F32).rearrange("p (q j w u) -> p q j w u", q=8 * nch, j=NJ, w=2, u=2)
            nc.vector.tensor_copy(
                out=xg_view[:, ja:jb, :, 8 * c0 : 8 * (c0 + nch), :],
                in_=xs_words[:, :, ja:jb].rearrange("p q j w u -> p j u q w"),
            )

        xc = keep.tile([P, 4096], U32, name="xc", align_bytes=64)
        xsc = keep.tile([P, 4096], U8, name="xsc", align_bytes=64)

        def x_transpose(u):
            ja, jb = units[u][1:]
            for j0 in range(ja, jb, 2):
                tp = psum.tile([P, 512], F32, name="tpx", tag="tp", bufs=2)
                tiles[("tpx", u, j0)] = tp
                for jj in range(2):
                    for h in range(2):
                        c0 = (j0 + jj) * 256 + h * P
                        nc.tensor.transpose(
                            tp[:, (2 * jj + h) * P : (2 * jj + h + 1) * P], xg[:, c0 : c0 + P], ident[:]
                        )

        def x_copy(u, *engines):
            ja, jb = units[u][1:]
            gx = work.tile([P, 2048], BF16, name="gx", tag="gx", bufs=2, align_bytes=64)
            tiles[("gx", u)] = gx
            gxw = gx[:].bitcast(F32).rearrange("p (h jj c u) -> p h jj c u", h=2, jj=2, c=P, u=2)
            for h in range((jb - ja) // 2):
                engines[h](
                    out=gxw[:, h],
                    in_=tiles[("tpx", u, ja + 2 * h)][:].rearrange("p (jj u c) -> p jj c u", jj=2, u=2),
                )

        def x_quantise(u):
            ja, jb = units[u][1:]
            nc.vector.quantize_mx(
                out=xc[:, P * ja : P * jb].bitcast(FP8X4),
                scales=xsc[:, P * ja : P * jb],
                in_=tiles[("gx", u)][:, 0 : 512 * (jb - ja)],
            )

        last = len(X_CHUNKS) - 1
        regroup(0, 0, NJ)
        bzf = keep.tile([P, P], F32, name="bzf")
        nc.vector.tensor_copy(out=bzf[:], in_=bz[:])
        bps = psum.tile([P, 512], F32, name="bps", tag="tp", bufs=2)
        nc.tensor.transpose(bps[:, 0:P], bzf[:], ident[:])
        consts = keep.tile([P, 12], F32, name="consts")
        nc.vector.tensor_copy(out=consts[:, 0:12], in_=bps[:, 0:12])
        cc = keep.tile([P, 8], F32, name="cc")
        wsum = keep.tile([P, 1], F32, name="wsum")
        nc.vector.tensor_tensor(out=cc[:, 0:4], in0=consts[:, 4:8], in1=consts[:, 8:12], op=MULT)
        nc.vector.tensor_tensor(out=wsum[:], in0=a0s, in1=a2s, op=ADD)
        nc.vector.tensor_scalar_add(out=wsum[:], in0=wsum[:], scalar1=1.0)
        nc.vector.tensor_scalar_mul(out=cc[:, 4:8], in0=cc[:, 0:4], scalar1=wsum[:])
        for chunk in range(1, last):
            regroup(chunk, 0, NJ)
        bqp = psum.tile([P, 512], F32, name="bqp", tag="tp", bufs=2)
        nc.tensor.transpose(bqp[:, 0:P], consts[:, 0:1].to_broadcast([P, P]), ident[:])
        bq = keep.tile([P, P], F32, name="bq")
        nc.scalar.copy(out=bq[:], in_=bqp[:, 0:P])

        kv_of = {}
        hj_of = {}
        os_of = {}

        def begin_block(fb):
            kv = work.tile([P, 34 * P], F32, name="kv", tag="kv", bufs=2)
            hj = work.tile([P, 33 * ROW], F32, name="hj", tag="hj", bufs=2)
            kv_of[fb] = kv
            hj_of[fb] = hj
            for s in (0, 33):
                nc.scalar.activation(
                    out=kv[:, s * P : (s + 1) * P], in_=zero[:, 0:P], func=IDENTITY, bias=cc[:, fb : fb + 1], scale=1.0
                )
            nc.scalar.activation(
                out=hj[:].rearrange("p (j c) -> p j c", c=ROW)[:, :, 0:PAD],
                in_=zero[:].rearrange("p (j c) -> p j c", c=PAD),
                func=IDENTITY,
                bias=cc[:, 4 + fb : 5 + fb],
                scale=1.0,
            )

        def hwin(u, off):
            fb, ja, jb = units[u]
            return hj_of[fb][:, off : off + NJ * ROW].rearrange("p (j c) -> p j c", c=ROW)[:, ja:jb, 0:P]

        def kwin(u, s):
            fb, ja, jb = units[u]
            return kv_of[fb][:, (ja + s) * P : (jb + s) * P].rearrange("p (j c) -> p j c", c=P)

        def width(u):
            return P * (units[u][2] - units[u][1])

        def mx(dst, lhsT, lhsT_scale, rhs, rhs_scale):
            nc.tensor.matmul_mx(
                out=dst,
                lhsT=lhsT.bitcast(FP8X4),
                lhsT_scale=lhsT_scale,
                rhs=rhs.bitcast(FP8X4),
                rhs_scale=rhs_scale,
                start=True,
                stop=True,
            )

        def direct(u):
            return units[u][0] == 0 and u % 2 == 1

        def pe_project(u):
            fb, ja, jb = units[u]
            for what, third, bufs in (("v", 2, 1), ("q", 0, 1), ("k", 1, 2)):
                ps = psum.tile([P, 512], F32, name=what + "ps", tag=what + "ps", bufs=bufs)
                tiles[(what, u)] = ps
                w = slice((3 * fb + third) * P, (3 * fb + third + 1) * P)
                if what == "q" and direct(u):
                    for j in range(ja, jb):
                        c = slice(P * j, P * (j + 1))
                        mx(ps[:, P * (j - ja) : P * (j - ja + 1)], xc[:, c], xsc[:, c], wc[:, w], wsc[:, w])
                else:
                    c = slice(P * ja, P * jb)
                    mx(ps[:, 0 : width(u)], wc[:, w], wsc[:, w], xc[:, c], xsc[:, c])

        def act_v_q(u):
            fb = units[u][0]
            n = width(u)
            for what, c in (("v", 8 + fb), ("q", fb))[: 1 if direct(u) else 2]:
                t = work.tile([P, 512], F32, name=what + "t", tag=what + "t", bufs=3)
                tiles[(what + "t", u)] = t
                nc.scalar.activation(
                    out=t[:, 0:n], in_=tiles[(what, u)][:, 0:n], func=IDENTITY, bias=consts[:, c : c + 1], scale=1.0
                )

        def dve_kv(u):
            fb, ja, jb = units[u]
            n = width(u)
            nc.vector.scalar_tensor_tensor(
                out=kv_of[fb][:, (1 + ja) * P : (1 + jb) * P],
                in0=tiles[("k", u)][:, 0:n],
                scalar=consts[:, 4 + fb : 5 + fb],
                in1=tiles[("vt", u)][:, 0:n],
                op0=ADD,
                op1=MULT,
            )

        def pe_q_transpose(u):
            qtp = psum.tile([P, 512], F32, name="qtp", tag="tp", bufs=2)
            tiles[("qtp", u)] = qtp
            for c0 in range(0, width(u), P):
                nc.tensor.transpose(qtp[:, c0 : c0 + P], tiles[("qt", u)][:, c0 : c0 + P], ident[:])

        def dve_q_bias(u):
            fb = units[u][0]
            qts = work.tile([P, 512], F32, name="qts", tag="qts", bufs=5)
            tiles[("qts", u)] = qts
            n = width(u)
            nc.vector.tensor_tensor(
                out=qts[:, 0:n].rearrange("p (q jj s) -> p q jj s", q=16, s=8),
                in0=tiles[("q", u)][:, 0:n].rearrange("p (jj q s) -> p q jj s", q=16, s=8),
                in1=bq[:, fb * P : (fb + 1) * P]
                .rearrange("p (q s) -> p q s", s=8)
                .unsqueeze(2)
                .to_broadcast([P, 16, n // P, 8]),
                op=ADD,
            )

        def act_q_copy(u):
            qts = work.tile([P, 512], F32, name="qts", tag="qts", bufs=5)
            tiles[("qts", u)] = qts
            n = width(u)
            nc.scalar.copy(
                out=qts[:, 0:n].rearrange("p (q jj s) -> p q jj s", q=16, s=8),
                in_=tiles[("qtp", u)][:, 0:n].rearrange("p (jj q s) -> p q jj s", q=16, s=8),
            )

        def dve_columns_left(u):
            nc.vector.scalar_tensor_tensor(
                out=hwin(u, PAD), in0=kwin(u, 0), scalar=a0s, in1=kwin(u, 1), op0=MULT, op1=ADD
            )

        def dve_columns_right(u):
            nc.vector.scalar_tensor_tensor(
                out=hwin(u, PAD), in0=kwin(u, 2), scalar=a2s, in1=hwin(u, PAD), op0=MULT, op1=ADD
            )

        def act_scale_up(u):
            t0 = work.tile([P, 512], F32, name="t0", tag="t0", bufs=2)
            tiles[("t0", u)] = t0
            nc.scalar.activation(
                out=t0[:, 0 : width(u)].rearrange("p (j c) -> p j c", c=P), in_=hwin(u, PAD - 4), func=COPY, scale=a0r
            )

        def gps_scale_down(u):
            t2 = work.tile([P, 512], F32, name="t2", tag="t2", bufs=2)
            tiles[("t2", u)] = t2
            nc.gpsimd.tensor_scalar(
                out=t2[:, 0 : width(u)].rearrange("p (j c) -> p j c", c=P),
                in0=hwin(u, PAD + 4),
                scalar1=a2r,
                scalar2=0.0,
                op0=MULT,
                op1=ADD,
            )

        def pe_rows(u):
            fb, ja, jb = units[u]
            stp = psum.tile([P, 512], F32, name="stp", tag="stp", bufs=2)
            tiles[("stp", u)] = stp
            t0 = tiles[("t0", u)]
            t2 = tiles[("t2", u)]
            for jj in range(jb - ja):
                cols = slice(jj * P, (jj + 1) * P)
                c0 = (ja + jj) * ROW + PAD
                for n, src in enumerate((hj_of[fb][:, c0 : c0 + P], t0[:, cols], t2[:, cols])):
                    nc.tensor.matmul(
                        out=stp[:, cols], lhsT=src, rhs=ident[:], is_transpose=True, start=n == 0, stop=n == 2
                    )

        def store(fb, ja, jb):
            ost = os_of[(fb, ja // 16)]
            for b in range(NB):
                for c in range(2):
                    nc.sync.dma_start(
                        out=out[b, 2 * fb + c].rearrange("(i r) w -> i r w", r=8)[:, :, 8 * ja : 8 * jb],
                        in_=ost[b:P:4, c * 1024 : (c + 1) * 1024].rearrange("p (r w) -> p r w", r=8)[
                            :, :, 8 * (ja % 16) : 8 * (ja % 16 + jb - ja)
                        ],
                    )

        def dve_final(u):
            fb, ja, jb = units[u]
            n = width(u)
            if ja % 16 == 0:
                ost = work.tile([P, 2048], F32, name="ost", tag="ost", bufs=2)
                os_of[(fb, ja // 16)] = ost
            nc.vector.tensor_tensor(
                out=os_of[(fb, ja // 16)][:].rearrange("p (q j s) -> p q j s", q=16, s=8)[
                    :, :, ja % 16 : ja % 16 + jb - ja, :
                ],
                in0=tiles[("stp", u)][:, 0:n].rearrange("p (jj q s) -> p q jj s", q=16, s=8),
                in1=tiles[("qts", u)][:, 0:n].rearrange("p (q jj s) -> p q jj s", q=16, s=8),
                op=MULT,
            )
            stores = LAST_STORES if fb == NF - 1 else STORES
            if jb in stores:
                store(fb, stores[jb], jb)

        regroup(last, 0, 2)
        x_transpose(0)
        x_copy(0, nc.scalar.copy)
        regroup(last, 2, 8)
        x_transpose(1)
        x_copy(1, nc.scalar.copy)
        x_quantise(0)
        regroup(last, 8, NJ)
        x_transpose(2)
        x_copy(2, nc.scalar.copy, nc.vector.tensor_copy)
        x_quantise(1)

        for s in range(-1, n_units + 3):
            if live(s + 1):
                if units[s + 1][1] == 0:
                    begin_block(units[s + 1][0])
                pe_project(s + 1)
            if live(s - 1):
                dve_columns_right(s - 1)
            if live(s):
                dve_columns_left(s)
            if live(s - 3):
                dve_final(s - 3)
            if live(s + 1):
                act_v_q(s + 1)
                dve_kv(s + 1)
                if direct(s + 1):
                    dve_q_bias(s + 1)
            if live(s) and not direct(s):
                pe_q_transpose(s)
            if live(s - 1):
                act_scale_up(s - 1)
                gps_scale_down(s - 1)
            if live(s - 2):
                pe_rows(s - 2)
            if 3 <= s + 3 < n_x:
                x_transpose(s + 3)
            if 2 <= s + 2 < n_x:
                x_quantise(s + 2)
            if live(s) and units[s][0] + 1 < NF and units[s][2] == 28:
                w_quantise(units[s][0] + 1)
            if live(s) and not direct(s):
                act_q_copy(s)
            if 3 <= s + 3 < n_x:
                x_copy(s + 3, nc.scalar.copy, nc.vector.tensor_copy if s < 2 else nc.scalar.copy)
            if live(s) and units[s][0] + 1 < NF and units[s][2] == 24:
                w_transpose(units[s][0] + 1)
